import numpy as np
import ml_dtypes


def mxq(x, axis, fmt="e4m3"):
    dtype, down = {"e4m3": (ml_dtypes.float8_e4m3fn, 7), "e5m2": (ml_dtypes.float8_e5m2, 14)}[fmt]
    v = np.moveaxis(np.asarray(x, np.float32).astype(ml_dtypes.bfloat16).astype(np.float64), axis, -1)
    blocks = v.reshape(v.shape[:-1] + (-1, 32))
    amax = np.abs(blocks).max(-1, keepdims=True)
    byte = np.maximum(np.where(amax > 0, np.frexp(amax)[1] - 1 + 127, 0) - down, 1)
    scale = np.exp2(byte - 127.0)
    codes = (blocks / scale).astype(np.float32).astype(dtype).astype(np.float64)
    return np.moveaxis((codes * scale).reshape(v.shape), -1, axis)


WIDE = False


def mx_kscale(k):
    if not WIDE:
        return np.ones(k)
    levels = np.array([10, -10, 5, -5, 0])
    if k % 512:
        return np.exp2(np.random.permutation(np.resize(levels, k // 32))).repeat(32)
    a = np.empty((k // 512, 16))
    for p in range(k // 512):
        a[p, :8] = np.random.permutation(np.resize(levels, 8))
        for g in range(8):
            far = levels[np.abs(levels - a[p, g]) >= 10]
            a[p, g + 8] = far[np.random.randint(len(far))]
    return np.exp2(a.ravel()).repeat(32)


BF16 = ml_dtypes.bfloat16


def bf(x):
    return np.asarray(x, np.float32).astype(BF16)


def f64(x):
    return np.asarray(x).astype(np.float64)


B, T, C, H = 4, 128, 2048, 16
D = C // H
ROPE_BASE = 10000.0


def rope_cos_sin():
    inv_freq = 1.0 / (ROPE_BASE ** (np.arange(0, D, 2) / D))
    freqs = np.outer(np.arange(T) * 1.0, inv_freq)
    emb = np.concatenate([freqs, freqs], axis=-1)
    return np.cos(emb), np.sin(emb)


def rotate_half(v):
    v1, v2 = np.split(v, 2, axis=-1)
    return np.concatenate([-v2, v1], axis=-1)


def apply_rotary(v, cos, sin):
    return v * cos[None, None] + rotate_half(v) * sin[None, None]


def draw0():
    s = mx_kscale(C)
    return {"x": bf(np.random.standard_normal((B, T, C)) * s),
            "W_qk": bf(np.random.standard_normal((C, 2 * C)) / np.sqrt(C) / s[:, None]),
            "b_qk": bf(np.random.standard_normal(2 * C) * 0.3)}


def core(x, W_qk, b_qk):
    qk = (mxq(f64(x), 2, "e4m3") @ mxq(f64(W_qk), 0, "e4m3")) + f64(b_qk)
    q, k = np.split(qk, 2, axis=2)
    q = q.reshape(B, T, H, D).transpose(0, 2, 1, 3)
    k = k.reshape(B, T, H, D).transpose(0, 2, 1, 3)
    cos, sin = rope_cos_sin()
    return apply_rotary(q, cos, sin), apply_rotary(k, cos, sin)


def e4m3fn_bytes(y):
    return np.clip(np.asarray(y, np.float64), -448.0, 448.0).astype(np.float32).astype(ml_dtypes.float8_e4m3fn).view(np.uint8)


def e4m3fn_values(b):
    return np.asarray(b, np.uint8).view(ml_dtypes.float8_e4m3fn).astype(np.float64)


def setup_inputs():
    d = draw0()
    x0 = np.asarray(d['W_qk']).astype(np.float64)
    s = (np.max(np.abs(x0), axis=(1,), keepdims=True) / 448.0).astype(np.float32)
    out = {}
    for k, v in d.items():
        if k == 'W_qk':
            out['W_qk_bytes'] = e4m3fn_bytes(x0 / s.astype(np.float64))
            out['W_qk_scale'] = s
        else:
            out[k] = v
    return out


def reference(x, W_qk_bytes, W_qk_scale, b_qk):
    return core(x, e4m3fn_values(W_qk_bytes) * W_qk_scale.astype(np.float64), b_qk)

@@ -1,0 +1,287 @@
+import math
+from contextlib import ExitStack
+
+import concourse.mybir as mybir
+from concourse.masks import make_identity
+
+FLOPS = 2 * 512 * 2048 * 4096
+
+F32 = mybir.dt.float32
+BF16 = mybir.dt.bfloat16
+I32 = mybir.dt.int32
+U32 = mybir.dt.uint32
+U8 = mybir.dt.uint8
+FP8 = mybir.dt.float8_e4m3fn
+FP8X4 = mybir.dt.float8_e4m3fn_x4
+ALU = mybir.AluOpType
+ACT = mybir.ActivationFunctionType
+
+P = 128
+PACK = 4
+PASSES = 4
+BATCH = 4
+T = 128
+D = 128
+TOK = BATCH * T
+HEADS = 32
+GROUP_HEADS = (2, 2, 4, 4, 4, 4, 4, 4, 2, 2)
+MM_AHEAD = 2
+EVAC_LAG = 2
+X_STEP = 6
+
+TWO_PI = 2.0 * math.pi
+C1 = 6.28125
+C2 = 0.0019350051879882812
+C3 = TWO_PI - C1 - C2
+
+
+def tile_causalselfattention_pa_kernel(tc, x, W_qk_bytes, W_qk_scale, b_qk, out_0, out_1):
+    nc = tc.nc
+    chunks = [(n, g) for n in range(len(GROUP_HEADS)) for g in range(PASSES)]
+    n_chunks = len(chunks)
+    first_head = [sum(GROUP_HEADS[:n]) for n in range(len(GROUP_HEADS))]
+    head_group = [n for n in range(len(GROUP_HEADS)) for i in range(GROUP_HEADS[n])]
+
+    with ExitStack() as ctx:
+        const = ctx.enter_context(tc.tile_pool(name="const", bufs=1))
+        wbytes = ctx.enter_context(tc.tile_pool(name="wbytes", bufs=1))
+        work = ctx.enter_context(tc.tile_pool(name="work", bufs=2))
+        psum_acc = ctx.enter_context(tc.psum_pool(name="psum_acc", bufs=4))
+        psum_tr = ctx.enter_context(tc.psum_pool(name="psum_tr", bufs=4))
+        ctx.enter_context(tc.manual_schedule())
+
+        w_view = W_qk_bytes.rearrange("(g p t) n -> g p t n", p=P, t=PACK)
+        x_view = x.rearrange("b t (g k) -> g t b k", g=PASSES)
+
+        wsc = const.tile([P, PASSES, PACK], F32, name="wsc")
+        nc.sync.dma_start(out=wsc[:], in_=W_qk_scale.rearrange("(g p t) o -> p g (t o)", p=P, t=PACK))
+
+        bias_raw = const.tile([P, D], BF16, name="bias_raw")
+        nc.gpsimd.memset(bias_raw[:], 0.0)
+        nc.gpsimd.dma_start(out=bias_raw[0:HEADS, :], in_=b_qk.rearrange("(c d) -> c d", d=D))
+
+        wb = {}
+        x_sb = {}
+
+        def load_w(n):
+            cols = GROUP_HEADS[n] * D
+            c0 = first_head[n] * D
+            for g in range(PASSES):
+                wb[(n, g)] = wbytes.tile([P, PACK, cols], U8, name="wb_%d_%d" % (n, g))
+                nc.sync.dma_start(out=wb[(n, g)][:], in_=w_view[g][:, :, c0:c0 + cols])
+
+        def load_x(g):
+            x_sb[g] = const.tile([P, BATCH, 512], BF16, name="x_sb_%d" % g)
+            nc.sync.dma_start(out=x_sb[g][:], in_=x_view[g])
+
+        load_w(0)
+        load_x(0)
+        load_x(1)
+        load_w(1)
+        load_x(2)
+        load_x(3)
+        for n in range(2, len(GROUP_HEADS)):
+            load_w(n)
+
+        zero1 = const.tile([P, 1], F32, name="zero1")
+        nc.gpsimd.memset(zero1[:], 0.0)
+        junk1 = const.tile([P, 1], F32, name="junk1")
+        nc.scalar.activation(out=junk1[:], in_=zero1[:], func=ACT.Sin)
+
+        d_i = const.tile([P, 7], I32, name="d_i")
+        nc.gpsimd.iota(d_i[:], pattern=[[0, 7]], base=0, channel_multiplier=1)
+        m_i = const.tile([P, 7], I32, name="m_i")
+        nc.gpsimd.iota(m_i[:], pattern=[[1, 7]], base=0, channel_multiplier=0)
+        t_i = const.tile([P, T], I32, name="t_i")
+        nc.gpsimd.iota(t_i[:], pattern=[[1, T]], base=0, channel_multiplier=0)
+        ident2 = const.tile([P, D + D // 2], F32, name="ident2")
+        make_identity(nc, ident2[:, 0:D])
+        nc.gpsimd.tensor_copy(out=ident2[:, D:D + D // 2], in_=ident2[:, 0:D // 2])
+        ident = ident2[:, 0:D]
+        swap = ident2[:, D // 2:D + D // 2]
+
+        sh_i = const.tile([P, 7], I32, name="sh_i")
+        nc.vector.tensor_tensor(out=sh_i[:], in0=d_i[:], in1=m_i[:], op=ALU.logical_shift_right)
+        bit_i = const.tile([P, 7], I32, name="bit_i")
+        nc.vector.tensor_single_scalar(out=bit_i[:], in_=sh_i[:], scalar=1, op=ALU.bitwise_and)
+        bit_f = const.tile([P, 7], F32, name="bit_f")
+        nc.vector.tensor_copy(out=bit_f[:], in_=bit_i[:])
+        nbit_f = const.tile([P, 7], F32, name="nbit_f")
+        nc.vector.tensor_scalar(out=nbit_f[:], in0=bit_f[:], scalar1=-1.0, scalar2=1.0, op0=ALU.mult, op1=ALU.add)
+        fac = const.tile([P, 6], F32, name="fac")
+        for m in range(6):
+            nc.vector.scalar_tensor_tensor(
+                out=fac[:, m:m + 1], in0=bit_f[:, m:m + 1], scalar=10000.0 ** (-(2.0 ** m) / 64.0),
+                in1=nbit_f[:, m:m + 1], op0=ALU.mult, op1=ALU.add)
+        om1 = const.tile([P, 1], F32, name="om1")
+        nc.vector.tensor_scalar(out=om1[:], in0=fac[:, 0:1], scalar1=fac[:, 1:2], scalar2=fac[:, 2:3],
+                                op0=ALU.mult, op1=ALU.mult)
+        om2 = const.tile([P, 1], F32, name="om2")
+        nc.vector.tensor_scalar(out=om2[:], in0=om1[:], scalar1=fac[:, 3:4], scalar2=fac[:, 4:5],
+                                op0=ALU.mult, op1=ALU.mult)
+        omega = const.tile([P, 1], F32, name="omega")
+        nc.vector.tensor_scalar(out=omega[:], in0=om2[:], scalar1=fac[:, 5:6], scalar2=None, op0=ALU.mult)
+        sgn = const.tile([P, 1], F32, name="sgn")
+        nc.vector.tensor_scalar(out=sgn[:], in0=bit_f[:, 6:7], scalar1=-2.0, scalar2=1.0, op0=ALU.mult, op1=ALU.add)
+        t_f = const.tile([P, T], F32, name="t_f")
+        nc.vector.tensor_copy(out=t_f[:], in_=t_i[:])
+        theta = const.tile([P, T], F32, name="theta")
+        nc.vector.tensor_scalar(out=theta[:], in0=t_f[:], scalar1=omega[:, 0:1], scalar2=None, op0=ALU.mult)
+        k_i = const.tile([P, T], I32, name="k_i")
+        nc.vector.tensor_scalar(out=k_i[:], in0=theta[:], scalar1=1.0 / TWO_PI, scalar2=None, op0=ALU.mult)
+        k_f = const.tile([P, T], F32, name="k_f")
+        nc.vector.tensor_copy(out=k_f[:], in_=k_i[:])
+        ph = [const.tile([P, T], F32, name="ph_%d" % i) for i in range(5)]
+        nc.vector.scalar_tensor_tensor(out=ph[0][:], in0=k_f[:], scalar=-C1, in1=theta[:], op0=ALU.mult, op1=ALU.add)
+        nc.vector.scalar_tensor_tensor(out=ph[1][:], in0=k_f[:], scalar=-C2, in1=ph[0][:], op0=ALU.mult, op1=ALU.add)
+        nc.vector.scalar_tensor_tensor(out=ph[2][:], in0=k_f[:], scalar=-C3, in1=ph[1][:], op0=ALU.mult, op1=ALU.add)
+        over = const.tile([P, T], F32, name="over")
+        nc.vector.tensor_single_scalar(out=over[:], in_=ph[2][:], scalar=math.pi, op=ALU.is_gt)
+        nc.vector.scalar_tensor_tensor(out=ph[3][:], in0=over[:], scalar=-C1, in1=ph[2][:], op0=ALU.mult, op1=ALU.add)
+        nc.vector.scalar_tensor_tensor(out=ph[4][:], in0=over[:], scalar=-(C2 + C3), in1=ph[3][:],
+                                       op0=ALU.mult, op1=ALU.add)
+        phi = ph[4]
+        aphi = const.tile([P, T], F32, name="aphi")
+        nc.vector.scalar_tensor_tensor(out=aphi[:], in0=phi[:], scalar=-1.0, in1=phi[:], op0=ALU.mult, op1=ALU.max)
+        bias_f = const.tile([P, D], F32, name="bias_f")
+
+        cos_t = const.tile([P, BATCH, T], F32, name="cos_t")
+        sin_t = const.tile([P, BATCH, T], F32, name="sin_t")
+        bias_sb = const.tile([P, HEADS], F32, name="bias_sb")
+
+        def trig_tables():
+            for b in range(BATCH):
+                nc.scalar.activation(out=cos_t[:, b, :], in_=aphi[:], func=ACT.Sin, bias=math.pi / 2.0, scale=-1.0)
+                nc.scalar.activation(out=sin_t[:, b, :], in_=phi[:], func=ACT.Sin, scale=sgn[:, 0:1])
+
+        x_codes = const.tile([P, PASSES, TOK], U32, name="x_codes", align_bytes=64)
+        x_scl = const.tile([P, PASSES, TOK], U8, name="x_scl", align_bytes=64)
+
+        def x_path():
+            nc.vector.tensor_copy(out=bias_f[:], in_=bias_raw[:])
+            bt = psum_tr.tile([P, 512], F32, name="bt", tag="tr")
+            nc.tensor.transpose(out=bt[:, 0:D], in_=bias_f[:], identity=ident)
+            nc.vector.tensor_copy(out=bias_sb[:], in_=bt[:, 0:HEADS])
+            xg = {}
+            for g in range(PASSES):
+                xg[g] = const.tile([P, TOK, PACK], BF16, name="xg_%d" % g, align_bytes=64)
+                xg_w = xg[g][:].rearrange("p r j -> p (r j)").bitcast(F32).rearrange(
+                    "p (h b r u) -> p h b r u", h=2, b=2, u=2)
+                for half in range(2):
+                    xt = psum_tr.tile([P, 2, 2, T], F32, name="xt", tag="tr")
+                    for bb in range(2):
+                        words = x_sb[g][:, 2 * half + bb, :].bitcast(F32)
+                        for u in range(2):
+                            nc.tensor.transpose(out=xt[:, bb, u, :], in_=words[:, u:256:2], identity=ident)
+                    src = xt[:].rearrange("p b u r -> p b r u")
+                    if half == 0:
+                        nc.scalar.copy(out=xg_w[:, half], in_=src)
+                    else:
+                        nc.vector.tensor_copy(out=xg_w[:, half], in_=src)
+            for g in range(PASSES):
+                nc.vector.quantize_mx(out=x_codes[:, g, :].bitcast(FP8X4), scales=x_scl[:, g, :],
+                                      in_=xg[g][:].rearrange("p r j -> p (r j)"))
+
+        planes = {}
+        inter = {}
+        w_codes = {}
+        w_scl = {}
+
+        def widen(c):
+            n, g = chunks[c]
+            cols = GROUP_HEADS[n] * D
+            planes[c] = work.tile([P, PACK, cols], BF16, name="planes", tag="planes", bufs=3)
+            for t in range(PACK):
+                nc.scalar.activation(out=planes[c][:, t, :], in_=wb[(n, g)][:, t, :].bitcast(FP8), func=ACT.Copy,
+                                     scale=wsc[:, g, t:t + 1])
+
+        def interleave(c):
+            n, g = chunks[c]
+            cols = GROUP_HEADS[n] * D
+            inter[c] = work.tile([P, cols, PACK], BF16, name="inter", tag="inter", bufs=2, align_bytes=64)
+            nc.vector.tensor_copy(out=inter[c][:], in_=planes[c][:].rearrange("p t n -> p n t"))
+
+        def quantize(c):
+            n, g = chunks[c]
+            cols = GROUP_HEADS[n] * D
+            if g == 0:
+                w_codes[n] = work.tile([P, PASSES, cols], U32, name="w_codes", tag="w_codes", bufs=3, align_bytes=64)
+                w_scl[n] = work.tile([P, PASSES, cols], U8, name="w_scl", tag="w_scl", bufs=3, align_bytes=64)
+            nc.vector.quantize_mx(out=w_codes[n][:, g, :].bitcast(FP8X4), scales=w_scl[n][:, g, :],
+                                  in_=inter[c][:].rearrange("p n t -> p (n t)"))
+
+        acc = {}
+        rot_a = {}
+        rot_b = {}
+        turned = {}
+
+        def project(k):
+            n = head_group[k]
+            c0 = (k - first_head[n]) * D
+            acc[k] = psum_acc.tile([P, TOK], F32, name="acc", tag="acc")
+            for g in range(PASSES):
+                nc.tensor.matmul_mx(
+                    out=acc[k][:],
+                    lhsT=w_codes[n][:, g, c0:c0 + D].bitcast(FP8X4), lhsT_scale=w_scl[n][:, g, c0:c0 + D],
+                    rhs=x_codes[:, g, :].bitcast(FP8X4), rhs_scale=x_scl[:, g, :],
+                    start=(g == 0), stop=(g == PASSES - 1))
+
+        def rope(k):
+            rot_a[k] = work.tile([P, TOK], F32, name="rot_a", tag="rot_a", bufs=3)
+            rot_b[k] = work.tile([P, TOK], F32, name="rot_b", tag="rot_b", bufs=3)
+            nc.vector.scalar_tensor_tensor(out=rot_a[k][:], in0=acc[k][:], scalar=bias_sb[:, k:k + 1],
+                                           in1=cos_t[:].rearrange("p b t -> p (b t)"), op0=ALU.add, op1=ALU.mult)
+            nc.vector.scalar_tensor_tensor(out=rot_b[k][:], in0=acc[k][:], scalar=bias_sb[:, k:k + 1],
+                                           in1=sin_t[:].rearrange("p b t -> p (b t)"), op0=ALU.add, op1=ALU.mult)
+
+        def turn(k):
+            turned[k] = psum_tr.tile([P, BATCH, D], F32, name="turned", tag="tr")
+            for b in range(BATCH):
+                nc.tensor.matmul(out=turned[k][:, b, :], lhsT=rot_a[k][:, b * T:(b + 1) * T], rhs=ident,
+                                 is_transpose=True, start=True, stop=False)
+                nc.tensor.matmul(out=turned[k][:, b, :], lhsT=rot_b[k][:, b * T:(b + 1) * T], rhs=swap,
+                                 is_transpose=True, start=False, stop=True)
+
+        def leave(k):
+            o_sb = work.tile([P, BATCH, D], F32, name="o_sb", tag="o_sb", bufs=3)
+            nc.scalar.copy(out=o_sb[:], in_=turned[k][:])
+            dst = out_0 if k < HEADS // 2 else out_1
+            nc.sync.dma_start(out=dst[:, k % (HEADS // 2), :, :].rearrange("b t d -> t b d"), in_=o_sb[:])
+
+        state = {"ready": 0, "projected": 0, "slots": 0}
+
+        def slot():
+            k = state["slots"]
+            while state["projected"] < min(state["ready"], k + MM_AHEAD + 1):
+                project(state["projected"])
+                state["projected"] += 1
+            rope(k)
+            turn(k)
+            if k >= EVAC_LAG:
+                leave(k - EVAC_LAG)
+            state["slots"] += 1
+
+        for s in range(n_chunks + 2):
+            if s == 2:
+                trig_tables()
+            if s == X_STEP:
+                x_path()
+            if s < n_chunks:
+                widen(s)
+            if 1 <= s <= n_chunks:
+                interleave(s - 1)
+            if s >= 2:
+                quantize(s - 2)
+                n, g = chunks[s - 2]
+                if g == PASSES - 1:
+                    state["ready"] += GROUP_HEADS[n]
+            due = 0
+            for n in range(len(GROUP_HEADS)):
+                last = PASSES * n + PASSES - 1
+                due += (GROUP_HEADS[n] * min(max(s - (last + 2), 0), PASSES)) // PASSES
+            while state["slots"] < due:
+                slot()
+        while state["slots"] < HEADS:
+            slot()
+        for k in range(HEADS - EVAC_LAG, HEADS):
+            leave(k)

@@ -28,6 +28,7 @@ GROUP_HEADS = (2, 2, 4, 4, 4, 4, 4, 4, 2, 2)
 MM_AHEAD = 2
 EVAC_LAG = 2
 X_STEP = 6
+G_COLS_PER_ROPE = 160
 
 TWO_PI = 2.0 * math.pi
 C1 = 6.28125
@@ -190,16 +191,27 @@ def tile_causalselfattention_pa_kernel(tc, x, W_qk_bytes, W_qk_scale, b_qk, out_
         def widen(c):
             n, g = chunks[c]
             cols = GROUP_HEADS[n] * D
-            planes[c] = work.tile([P, PACK, cols], BF16, name="planes", tag="planes", bufs=3)
+            planes[c] = work.tile([P, PACK, cols], BF16, name="planes", tag="planes", bufs=4)
             for t in range(PACK):
                 nc.scalar.activation(out=planes[c][:, t, :], in_=wb[(n, g)][:, t, :].bitcast(FP8), func=ACT.Copy,
                                      scale=wsc[:, g, t:t + 1])
 
-        def interleave(c):
+        g_cols = {}
+
+        def interleave_g(c, ropes):
             n, g = chunks[c]
             cols = GROUP_HEADS[n] * D
             inter[c] = work.tile([P, cols, PACK], BF16, name="inter", tag="inter", bufs=2, align_bytes=64)
-            nc.vector.tensor_copy(out=inter[c][:], in_=planes[c][:].rearrange("p t n -> p n t"))
+            g_cols[c] = min(G_COLS_PER_ROPE * ropes, cols - 64)
+            if g_cols[c] > 0:
+                nc.gpsimd.tensor_scalar(out=inter[c][:, 0:g_cols[c], :],
+                                        in0=planes[c][:, :, 0:g_cols[c]].rearrange("p t n -> p n t"),
+                                        scalar1=1.0, scalar2=0.0, op0=ALU.mult, op1=ALU.add)
+
+        def interleave_v(c):
+            lo = g_cols[c]
+            nc.vector.tensor_copy(out=inter[c][:, lo:, :].rearrange("p (c i) t -> p c t i", i=4),
+                                  in_=planes[c][:, :, lo:].rearrange("p t (c i) -> p c t i", i=4))
 
         def quantize(c):
             n, g = chunks[c]
@@ -266,10 +278,12 @@ def tile_causalselfattention_pa_kernel(tc, x, W_qk_bytes, W_qk_scale, b_qk, out_
                 trig_tables()
             if s == X_STEP:
                 x_path()
-            if s < n_chunks:
-                widen(s)
+            if s == 0:
+                widen(0)
+            if s + 1 < n_chunks:
+                widen(s + 1)
             if 1 <= s <= n_chunks:
-                interleave(s - 1)
+                interleave_v(s - 1)
             if s >= 2:
                 quantize(s - 2)
                 n, g = chunks[s - 2]
@@ -279,6 +293,8 @@ def tile_causalselfattention_pa_kernel(tc, x, W_qk_bytes, W_qk_scale, b_qk, out_
             for n in range(len(GROUP_HEADS)):
                 last = PASSES * n + PASSES - 1
                 due += (GROUP_HEADS[n] * min(max(s - (last + 2), 0), PASSES)) // PASSES
+            if s < n_chunks:
+                interleave_g(s, due - state["slots"])
             while state["slots"] < due:
                 slot()
         while state["slots"] < HEADS:

@@ -24,11 +24,12 @@ T = 128
 D = 128
 TOK = BATCH * T
 HEADS = 32
-GROUP_HEADS = (2, 2, 4, 4, 4, 4, 4, 4, 2, 2)
-MM_AHEAD = 2
+GROUP_HEADS = (2, 2, 4, 4, 4, 4, 4, 4, 2, 1, 1)
+MM_AHEAD = 3
 EVAC_LAG = 2
 X_STEP = 6
 G_COLS_PER_ROPE = 160
+S_SHARE = 32
 
 TWO_PI = 2.0 * math.pi
 C1 = 6.28125
@@ -146,14 +147,13 @@ def tile_causalselfattention_pa_kernel(tc, x, W_qk_bytes, W_qk_scale, b_qk, out_
         nc.vector.scalar_tensor_tensor(out=aphi[:], in0=phi[:], scalar=-1.0, in1=phi[:], op0=ALU.mult, op1=ALU.max)
         bias_f = const.tile([P, D], F32, name="bias_f")
 
-        cos_t = const.tile([P, BATCH, T], F32, name="cos_t")
-        sin_t = const.tile([P, BATCH, T], F32, name="sin_t")
+        trig = const.tile([P, 2, BATCH, T], F32, name="trig")
         bias_sb = const.tile([P, HEADS], F32, name="bias_sb")
 
         def trig_tables():
             for b in range(BATCH):
-                nc.scalar.activation(out=cos_t[:, b, :], in_=aphi[:], func=ACT.Sin, bias=math.pi / 2.0, scale=-1.0)
-                nc.scalar.activation(out=sin_t[:, b, :], in_=phi[:], func=ACT.Sin, scale=sgn[:, 0:1])
+                nc.scalar.activation(out=trig[:, 0, b, :], in_=aphi[:], func=ACT.Sin, bias=math.pi / 2.0, scale=-1.0)
+                nc.scalar.activation(out=trig[:, 1, b, :], in_=phi[:], func=ACT.Sin, scale=sgn[:, 0:1])
 
         x_codes = const.tile([P, PASSES, TOK], U32, name="x_codes", align_bytes=64)
         x_scl = const.tile([P, PASSES, TOK], U8, name="x_scl", align_bytes=64)
@@ -175,10 +175,7 @@ def tile_causalselfattention_pa_kernel(tc, x, W_qk_bytes, W_qk_scale, b_qk, out_
                         for u in range(2):
                             nc.tensor.transpose(out=xt[:, bb, u, :], in_=words[:, u:256:2], identity=ident)
                     src = xt[:].rearrange("p b u r -> p b r u")
-                    if half == 0:
-                        nc.scalar.copy(out=xg_w[:, half], in_=src)
-                    else:
-                        nc.vector.tensor_copy(out=xg_w[:, half], in_=src)
+                    nc.scalar.copy(out=xg_w[:, half], in_=src)
             for g in range(PASSES):
                 nc.vector.quantize_mx(out=x_codes[:, g, :].bitcast(FP8X4), scales=x_scl[:, g, :],
                                       in_=xg[g][:].rearrange("p r j -> p (r j)"))
@@ -197,19 +194,26 @@ def tile_causalselfattention_pa_kernel(tc, x, W_qk_bytes, W_qk_scale, b_qk, out_
                                      scale=wsc[:, g, t:t + 1])
 
         g_cols = {}
+        s_cols = {}
 
         def interleave_g(c, ropes):
             n, g = chunks[c]
             cols = GROUP_HEADS[n] * D
             inter[c] = work.tile([P, cols, PACK], BF16, name="inter", tag="inter", bufs=2, align_bytes=64)
-            g_cols[c] = min(G_COLS_PER_ROPE * ropes, cols - 64)
-            if g_cols[c] > 0:
-                nc.gpsimd.tensor_scalar(out=inter[c][:, 0:g_cols[c], :],
-                                        in0=planes[c][:, :, 0:g_cols[c]].rearrange("p t n -> p n t"),
+            shared = cols >= 2 * D
+            g_cols[c] = min(G_COLS_PER_ROPE * ropes, cols - 64) if shared else 0
+            s_cols[c] = 0
+            lo = g_cols[c]
+            if lo > 0:
+                nc.gpsimd.tensor_scalar(out=inter[c][:, 0:lo, :],
+                                        in0=planes[c][:, :, 0:lo].rearrange("p t n -> p n t"),
                                         scalar1=1.0, scalar2=0.0, op0=ALU.mult, op1=ALU.add)
+            if s_cols[c] > 0:
+                nc.scalar.copy(out=inter[c][:, lo:lo + s_cols[c], :],
+                               in_=planes[c][:, :, lo:lo + s_cols[c]].rearrange("p t n -> p n t"))
 
         def interleave_v(c):
-            lo = g_cols[c]
+            lo = g_cols[c] + s_cols[c]
             nc.vector.tensor_copy(out=inter[c][:, lo:, :].rearrange("p (c i) t -> p c t i", i=4),
                                   in_=planes[c][:, :, lo:].rearrange("p t (c i) -> p c t i", i=4))
 
@@ -223,8 +227,7 @@ def tile_causalselfattention_pa_kernel(tc, x, W_qk_bytes, W_qk_scale, b_qk, out_
                                   in_=inter[c][:].rearrange("p n t -> p (n t)"))
 
         acc = {}
-        rot_a = {}
-        rot_b = {}
+        rot = {}
         turned = {}
 
         def project(k):
@@ -239,19 +242,17 @@ def tile_causalselfattention_pa_kernel(tc, x, W_qk_bytes, W_qk_scale, b_qk, out_
                     start=(g == 0), stop=(g == PASSES - 1))
 
         def rope(k):
-            rot_a[k] = work.tile([P, TOK], F32, name="rot_a", tag="rot_a", bufs=3)
-            rot_b[k] = work.tile([P, TOK], F32, name="rot_b", tag="rot_b", bufs=3)
-            nc.vector.scalar_tensor_tensor(out=rot_a[k][:], in0=acc[k][:], scalar=bias_sb[:, k:k + 1],
-                                           in1=cos_t[:].rearrange("p b t -> p (b t)"), op0=ALU.add, op1=ALU.mult)
-            nc.vector.scalar_tensor_tensor(out=rot_b[k][:], in0=acc[k][:], scalar=bias_sb[:, k:k + 1],
-                                           in1=sin_t[:].rearrange("p b t -> p (b t)"), op0=ALU.add, op1=ALU.mult)
+            rot[k] = work.tile([P, 2, TOK], F32, name="rot", tag="rot", bufs=3)
+            nc.vector.scalar_tensor_tensor(out=rot[k][:], in0=acc[k][:].unsqueeze(1).to_broadcast([P, 2, TOK]),
+                                           scalar=bias_sb[:, k:k + 1], in1=trig[:].rearrange("p c b t -> p c (b t)"),
+                                           op0=ALU.add, op1=ALU.mult)
 
         def turn(k):
             turned[k] = psum_tr.tile([P, BATCH, D], F32, name="turned", tag="tr")
             for b in range(BATCH):
-                nc.tensor.matmul(out=turned[k][:, b, :], lhsT=rot_a[k][:, b * T:(b + 1) * T], rhs=ident,
+                nc.tensor.matmul(out=turned[k][:, b, :], lhsT=rot[k][:, 0, b * T:(b + 1) * T], rhs=ident,
                                  is_transpose=True, start=True, stop=False)
-                nc.tensor.matmul(out=turned[k][:, b, :], lhsT=rot_b[k][:, b * T:(b + 1) * T], rhs=swap,
+                nc.tensor.matmul(out=turned[k][:, b, :], lhsT=rot[k][:, 1, b * T:(b + 1) * T], rhs=swap,
                                  is_transpose=True, start=False, stop=True)
 
         def leave(k):

@@ -27,9 +27,9 @@ HEADS = 32
 GROUP_HEADS = (2, 2, 4, 4, 4, 4, 4, 4, 2, 1, 1)
 MM_AHEAD = 3
 EVAC_LAG = 2
-X_STEP = 6
+LOAD_LEAD = 10
 G_COLS_PER_ROPE = 160
-S_SHARE = 32
+V_PLANE_EVERY = 2
 
 TWO_PI = 2.0 * math.pi
 C1 = 6.28125
@@ -58,44 +58,46 @@ def tile_causalselfattention_pa_kernel(tc, x, W_qk_bytes, W_qk_scale, b_qk, out_
         wsc = const.tile([P, PASSES, PACK], F32, name="wsc")
         nc.sync.dma_start(out=wsc[:], in_=W_qk_scale.rearrange("(g p t) o -> p g (t o)", p=P, t=PACK))
 
-        bias_raw = const.tile([P, D], BF16, name="bias_raw")
-        nc.gpsimd.memset(bias_raw[:], 0.0)
-        nc.gpsimd.dma_start(out=bias_raw[0:HEADS, :], in_=b_qk.rearrange("(c d) -> c d", d=D))
-
-        wb = {}
-        x_sb = {}
-
-        def load_w(n):
-            cols = GROUP_HEADS[n] * D
-            c0 = first_head[n] * D
-            for g in range(PASSES):
-                wb[(n, g)] = wbytes.tile([P, PACK, cols], U8, name="wb_%d_%d" % (n, g))
-                nc.sync.dma_start(out=wb[(n, g)][:], in_=w_view[g][:, :, c0:c0 + cols])
-
-        def load_x(g):
-            x_sb[g] = const.tile([P, BATCH, 512], BF16, name="x_sb_%d" % g)
-            nc.sync.dma_start(out=x_sb[g][:], in_=x_view[g])
-
-        load_w(0)
-        load_x(0)
-        load_x(1)
-        load_w(1)
-        load_x(2)
-        load_x(3)
-        for n in range(2, len(GROUP_HEADS)):
-            load_w(n)
-
-        zero1 = const.tile([P, 1], F32, name="zero1")
-        nc.gpsimd.memset(zero1[:], 0.0)
-        junk1 = const.tile([P, 1], F32, name="junk1")
-        nc.scalar.activation(out=junk1[:], in_=zero1[:], func=ACT.Sin)
-
         d_i = const.tile([P, 7], I32, name="d_i")
         nc.gpsimd.iota(d_i[:], pattern=[[0, 7]], base=0, channel_multiplier=1)
         m_i = const.tile([P, 7], I32, name="m_i")
         nc.gpsimd.iota(m_i[:], pattern=[[1, 7]], base=0, channel_multiplier=0)
         t_i = const.tile([P, T], I32, name="t_i")
         nc.gpsimd.iota(t_i[:], pattern=[[1, T]], base=0, channel_multiplier=0)
+        zero1 = const.tile([P, 1], F32, name="zero1")
+        nc.gpsimd.memset(zero1[:], 0.0)
+        bias_raw = const.tile([P, D], BF16, name="bias_raw")
+        nc.gpsimd.memset(bias_raw[:], 0.0)
+
+        wb = {}
+        x_sb = {}
+
+        def load_w(c):
+            n, g = chunks[c]
+            cols = GROUP_HEADS[n] * D
+            c0 = first_head[n] * D
+            wb[(n, g)] = wbytes.tile([P, PACK, cols], U8, name="wb_%d_%d" % (n, g))
+            nc.sync.dma_start(out=wb[(n, g)][:], in_=w_view[g][:, :, c0:c0 + cols])
+
+        def load_x(g):
+            x_sb[g] = const.tile([P, BATCH, 512], BF16, name="x_sb_%d" % g)
+            nc.sync.dma_start(out=x_sb[g][:], in_=x_view[g])
+
+        for c in range(0, 4):
+            load_w(c)
+        nc.sync.dma_start(out=bias_raw[0:HEADS, :], in_=b_qk.rearrange("(c d) -> c d", d=D))
+        load_x(0)
+        load_x(1)
+        for c in range(4, 8):
+            load_w(c)
+        load_x(2)
+        load_x(3)
+        for c in range(8, LOAD_LEAD):
+            load_w(c)
+
+        junk1 = const.tile([P, 1], F32, name="junk1")
+        nc.scalar.activation(out=junk1[:], in_=zero1[:], func=ACT.Sin)
+
         ident2 = const.tile([P, D + D // 2], F32, name="ident2")
         make_identity(nc, ident2[:, 0:D])
         nc.gpsimd.tensor_copy(out=ident2[:, D:D + D // 2], in_=ident2[:, 0:D // 2])
@@ -158,27 +160,32 @@ def tile_causalselfattention_pa_kernel(tc, x, W_qk_bytes, W_qk_scale, b_qk, out_
         x_codes = const.tile([P, PASSES, TOK], U32, name="x_codes", align_bytes=64)
         x_scl = const.tile([P, PASSES, TOK], U8, name="x_scl", align_bytes=64)
 
-        def x_path():
+        xg = {}
+        bias_t = {}
+
+        def bias_turn():
             nc.vector.tensor_copy(out=bias_f[:], in_=bias_raw[:])
-            bt = psum_tr.tile([P, 512], F32, name="bt", tag="tr")
-            nc.tensor.transpose(out=bt[:, 0:D], in_=bias_f[:], identity=ident)
-            nc.vector.tensor_copy(out=bias_sb[:], in_=bt[:, 0:HEADS])
-            xg = {}
-            for g in range(PASSES):
-                xg[g] = const.tile([P, TOK, PACK], BF16, name="xg_%d" % g, align_bytes=64)
-                xg_w = xg[g][:].rearrange("p r j -> p (r j)").bitcast(F32).rearrange(
-                    "p (h b r u) -> p h b r u", h=2, b=2, u=2)
-                for half in range(2):
-                    xt = psum_tr.tile([P, 2, 2, T], F32, name="xt", tag="tr")
-                    for bb in range(2):
-                        words = x_sb[g][:, 2 * half + bb, :].bitcast(F32)
-                        for u in range(2):
-                            nc.tensor.transpose(out=xt[:, bb, u, :], in_=words[:, u:256:2], identity=ident)
-                    src = xt[:].rearrange("p b u r -> p b r u")
-                    nc.scalar.copy(out=xg_w[:, half], in_=src)
-            for g in range(PASSES):
-                nc.vector.quantize_mx(out=x_codes[:, g, :].bitcast(FP8X4), scales=x_scl[:, g, :],
-                                      in_=xg[g][:].rearrange("p r j -> p (r j)"))
+            bias_t[0] = psum_tr.tile([P, 512], F32, name="bt", tag="tr")
+            nc.tensor.transpose(out=bias_t[0][:, 0:D], in_=bias_f[:], identity=ident)
+
+        def bias_keep():
+            nc.vector.tensor_copy(out=bias_sb[:], in_=bias_t[0][:, 0:HEADS])
+
+        def x_turn(g):
+            xg[g] = const.tile([P, TOK, PACK], BF16, name="xg_%d" % g, align_bytes=64)
+            xg_w = xg[g][:].rearrange("p r j -> p (r j)").bitcast(F32).rearrange(
+                "p (h b r u) -> p h b r u", h=2, b=2, u=2)
+            for half in range(2):
+                xt = psum_tr.tile([P, 2, 2, T], F32, name="xt", tag="tr")
+                for bb in range(2):
+                    words = x_sb[g][:, 2 * half + bb, :].bitcast(F32)
+                    for u in range(2):
+                        nc.tensor.transpose(out=xt[:, bb, u, :], in_=words[:, u:256:2], identity=ident)
+                nc.scalar.copy(out=xg_w[:, half], in_=xt[:].rearrange("p b u r -> p b r u"))
+
+        def x_quant(g):
+            nc.vector.quantize_mx(out=x_codes[:, g, :].bitcast(FP8X4), scales=x_scl[:, g, :],
+                                  in_=xg[g][:].rearrange("p r j -> p (r j)"))
 
         planes = {}
         inter = {}
@@ -189,9 +196,13 @@ def tile_causalselfattention_pa_kernel(tc, x, W_qk_bytes, W_qk_scale, b_qk, out_
             n, g = chunks[c]
             cols = GROUP_HEADS[n] * D
             planes[c] = work.tile([P, PACK, cols], BF16, name="planes", tag="planes", bufs=4)
-            for t in range(PACK):
+            v_planes = 1 if (c < 8 or c % 4 == 0) else 0
+            for t in range(PACK - v_planes):
                 nc.scalar.activation(out=planes[c][:, t, :], in_=wb[(n, g)][:, t, :].bitcast(FP8), func=ACT.Copy,
                                      scale=wsc[:, g, t:t + 1])
+            for t in range(PACK - v_planes, PACK):
+                nc.vector.tensor_scalar(out=planes[c][:, t, :], in0=wb[(n, g)][:, t, :].bitcast(FP8),
+                                        scalar1=wsc[:, g, t:t + 1], scalar2=None, op0=ALU.mult)
 
         g_cols = {}
         s_cols = {}
@@ -256,7 +267,7 @@ def tile_causalselfattention_pa_kernel(tc, x, W_qk_bytes, W_qk_scale, b_qk, out_
                                  is_transpose=True, start=False, stop=True)
 
         def leave(k):
-            o_sb = work.tile([P, BATCH, D], F32, name="o_sb", tag="o_sb", bufs=3)
+            o_sb = work.tile([P, BATCH, D], F32, name="o_sb", tag="o_sb", bufs=4)
             nc.scalar.copy(out=o_sb[:], in_=turned[k][:])
             dst = out_0 if k < HEADS // 2 else out_1
             nc.sync.dma_start(out=dst[:, k % (HEADS // 2), :, :].rearrange("b t d -> t b d"), in_=o_sb[:])
@@ -275,14 +286,17 @@ def tile_causalselfattention_pa_kernel(tc, x, W_qk_bytes, W_qk_scale, b_qk, out_
             state["slots"] += 1
 
         for s in range(n_chunks + 2):
-            if s == 2:
-                trig_tables()
-            if s == X_STEP:
-                x_path()
+            if s + LOAD_LEAD < n_chunks:
+                load_w(s + LOAD_LEAD)
             if s == 0:
                 widen(0)
             if s + 1 < n_chunks:
                 widen(s + 1)
+            if s == 1:
+                trig_tables()
+                bias_turn()
+            if 2 <= s < 2 + PASSES:
+                x_turn(s - 2)
             if 1 <= s <= n_chunks:
                 interleave_v(s - 1)
             if s >= 2:
@@ -290,6 +304,10 @@ def tile_causalselfattention_pa_kernel(tc, x, W_qk_bytes, W_qk_scale, b_qk, out_
                 n, g = chunks[s - 2]
                 if g == PASSES - 1:
                     state["ready"] += GROUP_HEADS[n]
+            if s == 2:
+                bias_keep()
+            if 3 <= s < 3 + PASSES:
+                x_quant(s - 3)
             due = 0
             for n in range(len(GROUP_HEADS)):
                 last = PASSES * n + PASSES - 1

@@ -28,7 +28,7 @@ GROUP_HEADS = (2, 2, 4, 4, 4, 4, 4, 4, 2, 1, 1)
 MM_AHEAD = 3
 EVAC_LAG = 2
 LOAD_LEAD = 10
-G_COLS_PER_ROPE = 160
+G_COLS = (0, 152, 304)
 V_PLANE_EVERY = 2
 
 TWO_PI = 2.0 * math.pi
@@ -196,7 +196,7 @@ def tile_causalselfattention_pa_kernel(tc, x, W_qk_bytes, W_qk_scale, b_qk, out_
             n, g = chunks[c]
             cols = GROUP_HEADS[n] * D
             planes[c] = work.tile([P, PACK, cols], BF16, name="planes", tag="planes", bufs=4)
-            v_planes = 1 if (c < 8 or c % 4 == 0) else 0
+            v_planes = 1 if (c < 8 or c % 6 == 0) else 0
             for t in range(PACK - v_planes):
                 nc.scalar.activation(out=planes[c][:, t, :], in_=wb[(n, g)][:, t, :].bitcast(FP8), func=ACT.Copy,
                                      scale=wsc[:, g, t:t + 1])
@@ -212,7 +212,7 @@ def tile_causalselfattention_pa_kernel(tc, x, W_qk_bytes, W_qk_scale, b_qk, out_
             cols = GROUP_HEADS[n] * D
             inter[c] = work.tile([P, cols, PACK], BF16, name="inter", tag="inter", bufs=2, align_bytes=64)
             shared = cols >= 2 * D
-            g_cols[c] = min(G_COLS_PER_ROPE * ropes, cols - 64) if shared else 0
+            g_cols[c] = min(G_COLS[ropes], cols - 64) if shared else 0
             s_cols[c] = 0
             lo = g_cols[c]
             if lo > 0:
@@ -241,48 +241,75 @@ def tile_causalselfattention_pa_kernel(tc, x, W_qk_bytes, W_qk_scale, b_qk, out_
         rot = {}
         turned = {}
 
-        def project(k):
+        def project(k, passes):
             n = head_group[k]
             c0 = (k - first_head[n]) * D
-            acc[k] = psum_acc.tile([P, TOK], F32, name="acc", tag="acc")
-            for g in range(PASSES):
+            if passes[0] == 0:
+                acc[k] = psum_acc.tile([P, TOK], F32, name="acc", tag="acc")
+            for g in passes:
                 nc.tensor.matmul_mx(
                     out=acc[k][:],
                     lhsT=w_codes[n][:, g, c0:c0 + D].bitcast(FP8X4), lhsT_scale=w_scl[n][:, g, c0:c0 + D],
                     rhs=x_codes[:, g, :].bitcast(FP8X4), rhs_scale=x_scl[:, g, :],
                     start=(g == 0), stop=(g == PASSES - 1))
 
-        def rope(k):
-            rot[k] = work.tile([P, 2, TOK], F32, name="rot", tag="rot", bufs=3)
-            nc.vector.scalar_tensor_tensor(out=rot[k][:], in0=acc[k][:].unsqueeze(1).to_broadcast([P, 2, TOK]),
-                                           scalar=bias_sb[:, k:k + 1], in1=trig[:].rearrange("p c b t -> p c (b t)"),
+        def rope(k, b0, b1):
+            if b0 == 0:
+                rot[k] = work.tile([P, 2, TOK], F32, name="rot", tag="rot", bufs=3)
+            lo, hi = b0 * T, b1 * T
+            nc.vector.scalar_tensor_tensor(out=rot[k][:, :, lo:hi],
+                                           in0=acc[k][:, lo:hi].unsqueeze(1).to_broadcast([P, 2, hi - lo]),
+                                           scalar=bias_sb[:, k:k + 1],
+                                           in1=trig[:].rearrange("p c b t -> p c (b t)")[:, :, lo:hi],
                                            op0=ALU.add, op1=ALU.mult)
 
-        def turn(k):
-            turned[k] = psum_tr.tile([P, BATCH, D], F32, name="turned", tag="tr")
-            for b in range(BATCH):
-                nc.tensor.matmul(out=turned[k][:, b, :], lhsT=rot[k][:, 0, b * T:(b + 1) * T], rhs=ident,
+        def turn(k, b0, b1, own_bank):
+            if b0 == 0 or own_bank:
+                turned[(k, b0)] = psum_tr.tile([P, BATCH, D], F32, name="turned", tag="tr")
+            bank = turned[(k, b0)] if own_bank else turned[(k, 0)]
+            for b in range(b0, b1):
+                nc.tensor.matmul(out=bank[:, b, :], lhsT=rot[k][:, 0, b * T:(b + 1) * T], rhs=ident,
                                  is_transpose=True, start=True, stop=False)
-                nc.tensor.matmul(out=turned[k][:, b, :], lhsT=rot[k][:, 1, b * T:(b + 1) * T], rhs=swap,
+                nc.tensor.matmul(out=bank[:, b, :], lhsT=rot[k][:, 1, b * T:(b + 1) * T], rhs=swap,
                                  is_transpose=True, start=False, stop=True)
 
-        def leave(k):
+        def leave(k, b0, b1):
             o_sb = work.tile([P, BATCH, D], F32, name="o_sb", tag="o_sb", bufs=4)
-            nc.scalar.copy(out=o_sb[:], in_=turned[k][:])
+            nc.scalar.copy(out=o_sb[:, b0:b1, :], in_=turned[(k, b0)][:, b0:b1, :])
             dst = out_0 if k < HEADS // 2 else out_1
-            nc.sync.dma_start(out=dst[:, k % (HEADS // 2), :, :].rearrange("b t d -> t b d"), in_=o_sb[:])
+            nc.sync.dma_start(out=dst[b0:b1, k % (HEADS // 2), :, :].rearrange("b t d -> t b d"), in_=o_sb[:, b0:b1, :])
 
         state = {"ready": 0, "projected": 0, "slots": 0}
 
         def slot():
             k = state["slots"]
+            ahead = []
             while state["projected"] < min(state["ready"], k + MM_AHEAD + 1):
-                project(state["projected"])
+                h = state["projected"]
+                if h <= k + 1:
+                    project(h, (0, 1, 2, 3))
+                else:
+                    ahead.append(h)
                 state["projected"] += 1
-            rope(k)
-            turn(k)
-            if k >= EVAC_LAG:
-                leave(k - EVAC_LAG)
+            for h in ahead:
+                project(h, (0, 1))
+            if k < HEADS - 1:
+                rope(k, 0, BATCH)
+                turn(k, 0, 2, False)
+                for h in ahead:
+                    project(h, (2, 3))
+                turn(k, 2, BATCH, False)
+                if k >= EVAC_LAG:
+                    leave(k - EVAC_LAG, 0, BATCH)
+            else:
+                rope(k, 0, 2)
+                turn(k, 0, 2, True)
+                leave(k - 2, 0, BATCH)
+                rope(k, 2, BATCH)
+                turn(k, 2, BATCH, True)
+                leave(k - 1, 0, BATCH)
+                leave(k, 0, 2)
+                leave(k, 2, BATCH)
             state["slots"] += 1
 
         for s in range(n_chunks + 2):
@@ -318,5 +345,3 @@ def tile_causalselfattention_pa_kernel(tc, x, W_qk_bytes, W_qk_scale, b_qk, out_
                 slot()
         while state["slots"] < HEADS:
             slot()
-        for k in range(HEADS - EVAC_LAG, HEADS):
-            leave(k)

@@ -28,8 +28,8 @@ GROUP_HEADS = (2, 2, 4, 4, 4, 4, 4, 4, 2, 1, 1)
 MM_AHEAD = 3
 EVAC_LAG = 2
 LOAD_LEAD = 10
-G_COLS = (0, 152, 304)
-V_PLANE_EVERY = 2
+G_COLS = (0, 152, 368)
+MERGE_HEADS = 4
 
 TWO_PI = 2.0 * math.pi
 C1 = 6.28125
@@ -39,8 +39,16 @@ C3 = TWO_PI - C1 - C2
 
 def tile_causalselfattention_pa_kernel(tc, x, W_qk_bytes, W_qk_scale, b_qk, out_0, out_1):
     nc = tc.nc
-    chunks = [(n, g) for n in range(len(GROUP_HEADS)) for g in range(PASSES)]
+    loads = [(n, g) for n in range(len(GROUP_HEADS)) for g in range(PASSES)]
+    chunks = []
+    for n in range(len(GROUP_HEADS)):
+        step = 2 if GROUP_HEADS[n] == MERGE_HEADS else 1
+        for g in range(0, PASSES, step):
+            chunks.append((n, tuple(range(g, g + step))))
     n_chunks = len(chunks)
+    group_chunks = [len([c for c in chunks if c[0] == n]) for n in range(len(GROUP_HEADS))]
+    last_chunk = [max([i for i in range(n_chunks) if chunks[i][0] == n]) for n in range(len(GROUP_HEADS))]
+    loads_through = [PASSES * chunks[c][0] + chunks[c][1][-1] + 1 for c in range(n_chunks)]
     first_head = [sum(GROUP_HEADS[:n]) for n in range(len(GROUP_HEADS))]
     head_group = [n for n in range(len(GROUP_HEADS)) for i in range(GROUP_HEADS[n])]
 
@@ -73,7 +81,7 @@ def tile_causalselfattention_pa_kernel(tc, x, W_qk_bytes, W_qk_scale, b_qk, out_
         x_sb = {}
 
         def load_w(c):
-            n, g = chunks[c]
+            n, g = loads[c]
             cols = GROUP_HEADS[n] * D
             c0 = first_head[n] * D
             wb[(n, g)] = wbytes.tile([P, PACK, cols], U8, name="wb_%d_%d" % (n, g))
@@ -193,26 +201,31 @@ def tile_causalselfattention_pa_kernel(tc, x, W_qk_bytes, W_qk_scale, b_qk, out_
         w_scl = {}
 
         def widen(c):
-            n, g = chunks[c]
+            n, passes = chunks[c]
             cols = GROUP_HEADS[n] * D
-            planes[c] = work.tile([P, PACK, cols], BF16, name="planes", tag="planes", bufs=4)
-            v_planes = 1 if (c < 8 or c % 6 == 0) else 0
-            for t in range(PACK - v_planes):
-                nc.scalar.activation(out=planes[c][:, t, :], in_=wb[(n, g)][:, t, :].bitcast(FP8), func=ACT.Copy,
-                                     scale=wsc[:, g, t:t + 1])
-            for t in range(PACK - v_planes, PACK):
-                nc.vector.tensor_scalar(out=planes[c][:, t, :], in0=wb[(n, g)][:, t, :].bitcast(FP8),
-                                        scalar1=wsc[:, g, t:t + 1], scalar2=None, op0=ALU.mult)
+            planes[c] = work.tile([P, PACK, len(passes) * cols], BF16, name="planes", tag="planes", bufs=4)
+            for i in range(len(passes)):
+                g = passes[i]
+                load = PASSES * n + g
+                v_planes = 1 if (load < 8 or load % 6 == 0) else 0
+                for t in range(PACK - v_planes):
+                    nc.scalar.activation(out=planes[c][:, t, i * cols:(i + 1) * cols],
+                                         in_=wb[(n, g)][:, t, :].bitcast(FP8), func=ACT.Copy,
+                                         scale=wsc[:, g, t:t + 1])
+                for t in range(PACK - v_planes, PACK):
+                    nc.vector.tensor_scalar(out=planes[c][:, t, i * cols:(i + 1) * cols],
+                                            in0=wb[(n, g)][:, t, :].bitcast(FP8),
+                                            scalar1=wsc[:, g, t:t + 1], scalar2=None, op0=ALU.mult)
 
         g_cols = {}
         s_cols = {}
 
         def interleave_g(c, ropes):
-            n, g = chunks[c]
-            cols = GROUP_HEADS[n] * D
+            n, passes = chunks[c]
+            cols = len(passes) * GROUP_HEADS[n] * D
             inter[c] = work.tile([P, cols, PACK], BF16, name="inter", tag="inter", bufs=2, align_bytes=64)
             shared = cols >= 2 * D
-            g_cols[c] = min(G_COLS[ropes], cols - 64) if shared else 0
+            g_cols[c] = min(G_COLS[min(ropes, 2)], cols - 64) if shared else 0
             s_cols[c] = 0
             lo = g_cols[c]
             if lo > 0:
@@ -229,12 +242,14 @@ def tile_causalselfattention_pa_kernel(tc, x, W_qk_bytes, W_qk_scale, b_qk, out_
                                   in_=planes[c][:, :, lo:].rearrange("p t (c i) -> p c t i", i=4))
 
         def quantize(c):
-            n, g = chunks[c]
+            n, passes = chunks[c]
             cols = GROUP_HEADS[n] * D
-            if g == 0:
+            g0, g1 = passes[0], passes[-1] + 1
+            if g0 == 0:
                 w_codes[n] = work.tile([P, PASSES, cols], U32, name="w_codes", tag="w_codes", bufs=3, align_bytes=64)
                 w_scl[n] = work.tile([P, PASSES, cols], U8, name="w_scl", tag="w_scl", bufs=3, align_bytes=64)
-            nc.vector.quantize_mx(out=w_codes[n][:, g, :].bitcast(FP8X4), scales=w_scl[n][:, g, :],
+            nc.vector.quantize_mx(out=w_codes[n][:, g0:g1, :].rearrange("p g c -> p (g c)").bitcast(FP8X4),
+                                  scales=w_scl[n][:, g0:g1, :].rearrange("p g c -> p (g c)"),
                                   in_=inter[c][:].rearrange("p n t -> p (n t)"))
 
         acc = {}
@@ -312,9 +327,11 @@ def tile_causalselfattention_pa_kernel(tc, x, W_qk_bytes, W_qk_scale, b_qk, out_
                 leave(k, 2, BATCH)
             state["slots"] += 1
 
+        state["loaded"] = LOAD_LEAD
         for s in range(n_chunks + 2):
-            if s + LOAD_LEAD < n_chunks:
-                load_w(s + LOAD_LEAD)
+            while state["loaded"] < min(len(loads), loads_through[min(s, n_chunks - 1)] + LOAD_LEAD):
+                load_w(state["loaded"])
+                state["loaded"] += 1
             if s == 0:
                 widen(0)
             if s + 1 < n_chunks:
@@ -328,8 +345,8 @@ def tile_causalselfattention_pa_kernel(tc, x, W_qk_bytes, W_qk_scale, b_qk, out_
                 interleave_v(s - 1)
             if s >= 2:
                 quantize(s - 2)
-                n, g = chunks[s - 2]
-                if g == PASSES - 1:
+                n, passes = chunks[s - 2]
+                if passes[-1] == PASSES - 1:
                     state["ready"] += GROUP_HEADS[n]
             if s == 2:
                 bias_keep()
@@ -337,8 +354,8 @@ def tile_causalselfattention_pa_kernel(tc, x, W_qk_bytes, W_qk_scale, b_qk, out_
                 x_quant(s - 3)
             due = 0
             for n in range(len(GROUP_HEADS)):
-                last = PASSES * n + PASSES - 1
-                due += (GROUP_HEADS[n] * min(max(s - (last + 2), 0), PASSES)) // PASSES
+                spread = group_chunks[min(n + 1, len(GROUP_HEADS) - 1)]
+                due += (GROUP_HEADS[n] * min(max(s - (last_chunk[n] + 2), 0), spread)) // spread
             if s < n_chunks:
                 interleave_g(s, due - state["slots"])
             while state["slots"] < due:

@@ -207,7 +207,7 @@ def tile_causalselfattention_pa_kernel(tc, x, W_qk_bytes, W_qk_scale, b_qk, out_
             for i in range(len(passes)):
                 g = passes[i]
                 load = PASSES * n + g
-                v_planes = 1 if (load < 8 or load % 6 == 0) else 0
+                v_planes = 1 if (load < 8 or load % (2 if len(passes) == 2 else 6) == 0) else 0
                 for t in range(PACK - v_planes):
                     nc.scalar.activation(out=planes[c][:, t, i * cols:(i + 1) * cols],
                                          in_=wb[(n, g)][:, t, :].bitcast(FP8), func=ACT.Copy,

@@ -28,7 +28,7 @@ GROUP_HEADS = (2, 2, 4, 4, 4, 4, 4, 4, 2, 1, 1)
 MM_AHEAD = 3
 EVAC_LAG = 2
 LOAD_LEAD = 10
-G_COLS = (0, 152, 368)
+G_COLS = (0, 144, 368)
 MERGE_HEADS = 4
 
 TWO_PI = 2.0 * math.pi
@@ -238,8 +238,8 @@ def tile_causalselfattention_pa_kernel(tc, x, W_qk_bytes, W_qk_scale, b_qk, out_
 
         def interleave_v(c):
             lo = g_cols[c] + s_cols[c]
-            nc.vector.tensor_copy(out=inter[c][:, lo:, :].rearrange("p (c i) t -> p c t i", i=4),
-                                  in_=planes[c][:, :, lo:].rearrange("p t (c i) -> p c t i", i=4))
+            nc.vector.tensor_copy(out=inter[c][:, lo:, :].rearrange("p (c i) t -> p c t i", i=8),
+                                  in_=planes[c][:, :, lo:].rearrange("p t (c i) -> p c t i", i=8))
 
         def quantize(c):
             n, passes = chunks[c]

@@ -200,14 +200,18 @@ def tile_causalselfattention_pa_kernel(tc, x, W_qk_bytes, W_qk_scale, b_qk, out_
         w_codes = {}
         w_scl = {}
 
-        def widen(c):
+        def widen(c, spare):
             n, passes = chunks[c]
             cols = GROUP_HEADS[n] * D
             planes[c] = work.tile([P, PACK, len(passes) * cols], BF16, name="planes", tag="planes", bufs=4)
             for i in range(len(passes)):
                 g = passes[i]
                 load = PASSES * n + g
-                v_planes = 1 if (load < 8 or load % (2 if len(passes) == 2 else 6) == 0) else 0
+                v_planes = 1 if (load < 8 or load % 6 == 0) else 0
+                if load < 8 and load % 2 == 0:
+                    v_planes = 2
+                if len(passes) == 2:
+                    v_planes += (spare + 1 - i) // 2
                 for t in range(PACK - v_planes):
                     nc.scalar.activation(out=planes[c][:, t, i * cols:(i + 1) * cols],
                                          in_=wb[(n, g)][:, t, :].bitcast(FP8), func=ACT.Copy,
@@ -224,8 +228,7 @@ def tile_causalselfattention_pa_kernel(tc, x, W_qk_bytes, W_qk_scale, b_qk, out_
             n, passes = chunks[c]
             cols = len(passes) * GROUP_HEADS[n] * D
             inter[c] = work.tile([P, cols, PACK], BF16, name="inter", tag="inter", bufs=2, align_bytes=64)
-            shared = cols >= 2 * D
-            g_cols[c] = min(G_COLS[min(ropes, 2)], cols - 64) if shared else 0
+            g_cols[c] = min(G_COLS[min(ropes, 2)], cols)
             s_cols[c] = 0
             lo = g_cols[c]
             if lo > 0:
@@ -238,8 +241,9 @@ def tile_causalselfattention_pa_kernel(tc, x, W_qk_bytes, W_qk_scale, b_qk, out_
 
         def interleave_v(c):
             lo = g_cols[c] + s_cols[c]
-            nc.vector.tensor_copy(out=inter[c][:, lo:, :].rearrange("p (c i) t -> p c t i", i=8),
-                                  in_=planes[c][:, :, lo:].rearrange("p t (c i) -> p c t i", i=8))
+            if lo < inter[c].shape[1]:
+                nc.vector.tensor_copy(out=inter[c][:, lo:, :].rearrange("p (c i) t -> p c t i", i=8),
+                                      in_=planes[c][:, :, lo:].rearrange("p t (c i) -> p c t i", i=8))
 
         def quantize(c):
             n, passes = chunks[c]
@@ -327,15 +331,23 @@ def tile_causalselfattention_pa_kernel(tc, x, W_qk_bytes, W_qk_scale, b_qk, out_
                 leave(k, 2, BATCH)
             state["slots"] += 1
 
+        def ropes_due(s):
+            due = 0
+            for n in range(len(GROUP_HEADS)):
+                spread = group_chunks[min(n + 1, len(GROUP_HEADS) - 1)]
+                due += (GROUP_HEADS[n] * min(max(s - (last_chunk[n] + 2), 0), spread)) // spread
+            return due
+
         state["loaded"] = LOAD_LEAD
         for s in range(n_chunks + 2):
             while state["loaded"] < min(len(loads), loads_through[min(s, n_chunks - 1)] + LOAD_LEAD):
                 load_w(state["loaded"])
                 state["loaded"] += 1
+            due = ropes_due(s)
             if s == 0:
-                widen(0)
+                widen(0, 0)
             if s + 1 < n_chunks:
-                widen(s + 1)
+                widen(s + 1, (2 - min(due - state["slots"], 2)) if len(chunks[s][1]) == 2 else 0)
             if s == 1:
                 trig_tables()
                 bias_turn()
@@ -352,10 +364,6 @@ def tile_causalselfattention_pa_kernel(tc, x, W_qk_bytes, W_qk_scale, b_qk, out_
                 bias_keep()
             if 3 <= s < 3 + PASSES:
                 x_quant(s - 3)
-            due = 0
-            for n in range(len(GROUP_HEADS)):
-                spread = group_chunks[min(n + 1, len(GROUP_HEADS) - 1)]
-                due += (GROUP_HEADS[n] * min(max(s - (last_chunk[n] + 2), 0), spread)) // spread
             if s < n_chunks:
                 interleave_g(s, due - state["slots"])
             while state["slots"] < due:

@@ -135,24 +135,17 @@ def tile_causalselfattention_pa_kernel(tc, x, W_qk_bytes, W_qk_scale, b_qk, out_
         nc.vector.tensor_scalar(out=omega[:], in0=om2[:], scalar1=fac[:, 5:6], scalar2=None, op0=ALU.mult)
         sgn = const.tile([P, 1], F32, name="sgn")
         nc.vector.tensor_scalar(out=sgn[:], in0=bit_f[:, 6:7], scalar1=-2.0, scalar2=1.0, op0=ALU.mult, op1=ALU.add)
-        t_f = const.tile([P, T], F32, name="t_f")
-        nc.vector.tensor_copy(out=t_f[:], in_=t_i[:])
         theta = const.tile([P, T], F32, name="theta")
-        nc.vector.tensor_scalar(out=theta[:], in0=t_f[:], scalar1=omega[:, 0:1], scalar2=None, op0=ALU.mult)
+        nc.vector.tensor_scalar(out=theta[:], in0=t_i[:], scalar1=omega[:, 0:1], scalar2=None, op0=ALU.mult)
         k_i = const.tile([P, T], I32, name="k_i")
         nc.vector.tensor_scalar(out=k_i[:], in0=theta[:], scalar1=1.0 / TWO_PI, scalar2=None, op0=ALU.mult)
         k_f = const.tile([P, T], F32, name="k_f")
         nc.vector.tensor_copy(out=k_f[:], in_=k_i[:])
-        ph = [const.tile([P, T], F32, name="ph_%d" % i) for i in range(5)]
+        ph = [const.tile([P, T], F32, name="ph_%d" % i) for i in range(3)]
         nc.vector.scalar_tensor_tensor(out=ph[0][:], in0=k_f[:], scalar=-C1, in1=theta[:], op0=ALU.mult, op1=ALU.add)
         nc.vector.scalar_tensor_tensor(out=ph[1][:], in0=k_f[:], scalar=-C2, in1=ph[0][:], op0=ALU.mult, op1=ALU.add)
         nc.vector.scalar_tensor_tensor(out=ph[2][:], in0=k_f[:], scalar=-C3, in1=ph[1][:], op0=ALU.mult, op1=ALU.add)
-        over = const.tile([P, T], F32, name="over")
-        nc.vector.tensor_single_scalar(out=over[:], in_=ph[2][:], scalar=math.pi, op=ALU.is_gt)
-        nc.vector.scalar_tensor_tensor(out=ph[3][:], in0=over[:], scalar=-C1, in1=ph[2][:], op0=ALU.mult, op1=ALU.add)
-        nc.vector.scalar_tensor_tensor(out=ph[4][:], in0=over[:], scalar=-(C2 + C3), in1=ph[3][:],
-                                       op0=ALU.mult, op1=ALU.add)
-        phi = ph[4]
+        phi = ph[2]
         aphi = const.tile([P, T], F32, name="aphi")
         nc.vector.scalar_tensor_tensor(out=aphi[:], in0=phi[:], scalar=-1.0, in1=phi[:], op0=ALU.mult, op1=ALU.max)
         bias_f = const.tile([P, D], F32, name="bias_f")
@@ -350,6 +343,7 @@ def tile_causalselfattention_pa_kernel(tc, x, W_qk_bytes, W_qk_scale, b_qk, out_
                 widen(s + 1, (2 - min(due - state["slots"], 2)) if len(chunks[s][1]) == 2 else 0)
             if s == 1:
                 trig_tables()
+            if s == 6:
                 bias_turn()
             if 2 <= s < 2 + PASSES:
                 x_turn(s - 2)
@@ -360,7 +354,7 @@ def tile_causalselfattention_pa_kernel(tc, x, W_qk_bytes, W_qk_scale, b_qk, out_
                 n, passes = chunks[s - 2]
                 if passes[-1] == PASSES - 1:
                     state["ready"] += GROUP_HEADS[n]
-            if s == 2:
+            if s == 7:
                 bias_keep()
             if 3 <= s < 3 + PASSES:
                 x_quant(s - 3)

@@ -28,7 +28,7 @@ GROUP_HEADS = (2, 2, 4, 4, 4, 4, 4, 4, 2, 1, 1)
 MM_AHEAD = 3
 EVAC_LAG = 2
 LOAD_LEAD = 10
-G_COLS = (0, 144, 368)
+G_COLS = (0, 128, 336)
 MERGE_HEADS = 4
 
 TWO_PI = 2.0 * math.pi

@@ -298,10 +298,7 @@ def tile_causalselfattention_pa_kernel(tc, x, W_qk_bytes, W_qk_scale, b_qk, out_
             ahead = []
             while state["projected"] < min(state["ready"], k + MM_AHEAD + 1):
                 h = state["projected"]
-                if h <= k + 1:
-                    project(h, (0, 1, 2, 3))
-                else:
-                    ahead.append(h)
+                project(h, (0, 1, 2, 3))
                 state["projected"] += 1
             for h in ahead:
                 project(h, (0, 1))

@@ -28,6 +28,7 @@ GROUP_HEADS = (2, 2, 4, 4, 4, 4, 4, 4, 2, 1, 1)
 MM_AHEAD = 3
 EVAC_LAG = 2
 LOAD_LEAD = 10
+W_BUFS = 16
 G_COLS = (0, 128, 336)
 MERGE_HEADS = 4
 
@@ -54,7 +55,7 @@ def tile_causalselfattention_pa_kernel(tc, x, W_qk_bytes, W_qk_scale, b_qk, out_
 
     with ExitStack() as ctx:
         const = ctx.enter_context(tc.tile_pool(name="const", bufs=1))
-        wbytes = ctx.enter_context(tc.tile_pool(name="wbytes", bufs=1))
+        wbytes = ctx.enter_context(tc.tile_pool(name="wbytes", bufs=W_BUFS))
         work = ctx.enter_context(tc.tile_pool(name="work", bufs=2))
         psum_acc = ctx.enter_context(tc.psum_pool(name="psum_acc", bufs=4))
         psum_tr = ctx.enter_context(tc.psum_pool(name="psum_tr", bufs=4))
@@ -84,7 +85,7 @@ def tile_causalselfattention_pa_kernel(tc, x, W_qk_bytes, W_qk_scale, b_qk, out_
             n, g = loads[c]
             cols = GROUP_HEADS[n] * D
             c0 = first_head[n] * D
-            wb[(n, g)] = wbytes.tile([P, PACK, cols], U8, name="wb_%d_%d" % (n, g))
+            wb[(n, g)] = wbytes.tile([P, PACK, cols], U8, name="wb", tag="wb")
             nc.sync.dma_start(out=wb[(n, g)][:], in_=w_view[g][:, :, c0:c0 + cols])
 
         def load_x(g):
@@ -154,9 +155,10 @@ def tile_causalselfattention_pa_kernel(tc, x, W_qk_bytes, W_qk_scale, b_qk, out_
         bias_sb = const.tile([P, HEADS], F32, name="bias_sb")
 
         def trig_tables():
-            for b in range(BATCH):
-                nc.scalar.activation(out=trig[:, 0, b, :], in_=aphi[:], func=ACT.Sin, bias=math.pi / 2.0, scale=-1.0)
-                nc.scalar.activation(out=trig[:, 1, b, :], in_=phi[:], func=ACT.Sin, scale=sgn[:, 0:1])
+            nc.scalar.activation(out=trig[:, 0, :, :], in_=aphi[:].unsqueeze(1).to_broadcast([P, BATCH, T]), func=ACT.Sin,
+                                 bias=math.pi / 2.0, scale=-1.0)
+            nc.scalar.activation(out=trig[:, 1, :, :], in_=phi[:].unsqueeze(1).to_broadcast([P, BATCH, T]), func=ACT.Sin,
+                                 scale=sgn[:, 0:1])
 
         x_codes = const.tile([P, PASSES, TOK], U32, name="x_codes", align_bytes=64)
         x_scl = const.tile([P, PASSES, TOK], U8, name="x_scl", align_bytes=64)
@@ -196,7 +198,7 @@ def tile_causalselfattention_pa_kernel(tc, x, W_qk_bytes, W_qk_scale, b_qk, out_
         def widen(c, spare):
             n, passes = chunks[c]
             cols = GROUP_HEADS[n] * D
-            planes[c] = work.tile([P, PACK, len(passes) * cols], BF16, name="planes", tag="planes", bufs=4)
+            planes[c] = work.tile([P, PACK, len(passes) * cols], BF16, name="planes", tag="planes", bufs=8)
             for i in range(len(passes)):
                 g = passes[i]
                 load = PASSES * n + g
@@ -243,8 +245,8 @@ def tile_causalselfattention_pa_kernel(tc, x, W_qk_bytes, W_qk_scale, b_qk, out_
             cols = GROUP_HEADS[n] * D
             g0, g1 = passes[0], passes[-1] + 1
             if g0 == 0:
-                w_codes[n] = work.tile([P, PASSES, cols], U32, name="w_codes", tag="w_codes", bufs=3, align_bytes=64)
-                w_scl[n] = work.tile([P, PASSES, cols], U8, name="w_scl", tag="w_scl", bufs=3, align_bytes=64)
+                w_codes[n] = work.tile([P, PASSES, cols], U32, name="w_codes", tag="w_codes", bufs=4, align_bytes=64)
+                w_scl[n] = work.tile([P, PASSES, cols], U8, name="w_scl", tag="w_scl", bufs=4, align_bytes=64)
             nc.vector.quantize_mx(out=w_codes[n][:, g0:g1, :].rearrange("p g c -> p (g c)").bitcast(FP8X4),
                                   scales=w_scl[n][:, g0:g1, :].rearrange("p g c -> p (g c)"),
                                   in_=inter[c][:].rearrange("p n t -> p (n t)"))
@@ -267,7 +269,7 @@ def tile_causalselfattention_pa_kernel(tc, x, W_qk_bytes, W_qk_scale, b_qk, out_
 
         def rope(k, b0, b1):
             if b0 == 0:
-                rot[k] = work.tile([P, 2, TOK], F32, name="rot", tag="rot", bufs=3)
+                rot[k] = work.tile([P, 2, TOK], F32, name="rot", tag="rot", bufs=4)
             lo, hi = b0 * T, b1 * T
             nc.vector.scalar_tensor_tensor(out=rot[k][:, :, lo:hi],
                                            in0=acc[k][:, lo:hi].unsqueeze(1).to_broadcast([P, 2, hi - lo]),
@@ -286,7 +288,7 @@ def tile_causalselfattention_pa_kernel(tc, x, W_qk_bytes, W_qk_scale, b_qk, out_
                                  is_transpose=True, start=False, stop=True)
 
         def leave(k, b0, b1):
-            o_sb = work.tile([P, BATCH, D], F32, name="o_sb", tag="o_sb", bufs=4)
+            o_sb = work.tile([P, BATCH, D], F32, name="o_sb", tag="o_sb", bufs=6)
             nc.scalar.copy(out=o_sb[:, b0:b1, :], in_=turned[(k, b0)][:, b0:b1, :])
             dst = out_0 if k < HEADS // 2 else out_1
             nc.sync.dma_start(out=dst[b0:b1, k % (HEADS // 2), :, :].rearrange("b t d -> t b d"), in_=o_sb[:, b0:b1, :])

@@ -202,7 +202,7 @@ def tile_causalselfattention_pa_kernel(tc, x, W_qk_bytes, W_qk_scale, b_qk, out_
             for i in range(len(passes)):
                 g = passes[i]
                 load = PASSES * n + g
-                v_planes = 1 if (load < 8 or load % 6 == 0) else 0
+                v_planes = 1 if (load < 8 or (load % 4 == 0 and load < 32)) else 0
                 if load < 8 and load % 2 == 0:
                     v_planes = 2
                 if len(passes) == 2:
@@ -294,24 +294,25 @@ def tile_causalselfattention_pa_kernel(tc, x, W_qk_bytes, W_qk_scale, b_qk, out_
             nc.sync.dma_start(out=dst[b0:b1, k % (HEADS // 2), :, :].rearrange("b t d -> t b d"), in_=o_sb[:, b0:b1, :])
 
         state = {"ready": 0, "projected": 0, "slots": 0}
+        held = []
 
-        def slot():
+        def slot(hold):
             k = state["slots"]
             ahead = []
             while state["projected"] < min(state["ready"], k + MM_AHEAD + 1):
                 h = state["projected"]
                 project(h, (0, 1, 2, 3))
                 state["projected"] += 1
-            for h in ahead:
-                project(h, (0, 1))
             if k < HEADS - 1:
                 rope(k, 0, BATCH)
-                turn(k, 0, 2, False)
-                for h in ahead:
-                    project(h, (2, 3))
-                turn(k, 2, BATCH, False)
-                if k >= EVAC_LAG:
-                    leave(k - EVAC_LAG, 0, BATCH)
+                held.append(k)
+                if not hold:
+                    for h in held:
+                        turn(h, 0, BATCH, False)
+                    for h in held:
+                        if h >= EVAC_LAG:
+                            leave(h - EVAC_LAG, 0, BATCH)
+                    held.clear()
             else:
                 rope(k, 0, 2)
                 turn(k, 0, 2, True)
@@ -360,6 +361,6 @@ def tile_causalselfattention_pa_kernel(tc, x, W_qk_bytes, W_qk_scale, b_qk, out_
             if s < n_chunks:
                 interleave_g(s, due - state["slots"])
             while state["slots"] < due:
-                slot()
+                slot(state["slots"] + 1 < due)
         while state["slots"] < HEADS:
-            slot()
+            slot(False)

import math
from contextlib import ExitStack

import concourse.mybir as mybir
from concourse.masks import make_identity

FLOPS = 2 * 512 * 2048 * 4096

F32 = mybir.dt.float32
BF16 = mybir.dt.bfloat16
I32 = mybir.dt.int32
U32 = mybir.dt.uint32
U8 = mybir.dt.uint8
FP8 = mybir.dt.float8_e4m3fn
FP8X4 = mybir.dt.float8_e4m3fn_x4
ALU = mybir.AluOpType
ACT = mybir.ActivationFunctionType

P = 128
PACK = 4
PASSES = 4
BATCH = 4
T = 128
D = 128
TOK = BATCH * T
HEADS = 32
GROUP_HEADS = (2, 2, 4, 4, 4, 4, 4, 4, 2, 1, 1)
MM_AHEAD = 3
EVAC_LAG = 2
LOAD_LEAD = 10
W_BUFS = 16
G_COLS = (0, 128, 336)
MERGE_HEADS = 4

TWO_PI = 2.0 * math.pi
C1 = 6.28125
C2 = 0.0019350051879882812
C3 = TWO_PI - C1 - C2


def tile_causalselfattention_pa_kernel(tc, x, W_qk_bytes, W_qk_scale, b_qk, out_0, out_1):
    nc = tc.nc
    loads = [(n, g) for n in range(len(GROUP_HEADS)) for g in range(PASSES)]
    chunks = []
    for n in range(len(GROUP_HEADS)):
        step = 2 if GROUP_HEADS[n] == MERGE_HEADS else 1
        for g in range(0, PASSES, step):
            chunks.append((n, tuple(range(g, g + step))))
    n_chunks = len(chunks)
    group_chunks = [len([c for c in chunks if c[0] == n]) for n in range(len(GROUP_HEADS))]
    last_chunk = [max([i for i in range(n_chunks) if chunks[i][0] == n]) for n in range(len(GROUP_HEADS))]
    loads_through = [PASSES * chunks[c][0] + chunks[c][1][-1] + 1 for c in range(n_chunks)]
    first_head = [sum(GROUP_HEADS[:n]) for n in range(len(GROUP_HEADS))]
    head_group = [n for n in range(len(GROUP_HEADS)) for i in range(GROUP_HEADS[n])]

    with ExitStack() as ctx:
        const = ctx.enter_context(tc.tile_pool(name="const", bufs=1))
        wbytes = ctx.enter_context(tc.tile_pool(name="wbytes", bufs=W_BUFS))
        work = ctx.enter_context(tc.tile_pool(name="work", bufs=2))
        psum_acc = ctx.enter_context(tc.psum_pool(name="psum_acc", bufs=4))
        psum_tr = ctx.enter_context(tc.psum_pool(name="psum_tr", bufs=4))
        ctx.enter_context(tc.manual_schedule())

        w_view = W_qk_bytes.rearrange("(g p t) n -> g p t n", p=P, t=PACK)
        x_view = x.rearrange("b t (g k) -> g t b k", g=PASSES)

        wsc = const.tile([P, PASSES, PACK], F32, name="wsc")
        nc.sync.dma_start(out=wsc[:], in_=W_qk_scale.rearrange("(g p t) o -> p g (t o)", p=P, t=PACK))

        d_i = const.tile([P, 7], I32, name="d_i")
        nc.gpsimd.iota(d_i[:], pattern=[[0, 7]], base=0, channel_multiplier=1)
        m_i = const.tile([P, 7], I32, name="m_i")
        nc.gpsimd.iota(m_i[:], pattern=[[1, 7]], base=0, channel_multiplier=0)
        t_i = const.tile([P, T], I32, name="t_i")
        nc.gpsimd.iota(t_i[:], pattern=[[1, T]], base=0, channel_multiplier=0)
        zero1 = const.tile([P, 1], F32, name="zero1")
        nc.gpsimd.memset(zero1[:], 0.0)
        bias_raw = const.tile([P, D], BF16, name="bias_raw")
        nc.gpsimd.memset(bias_raw[:], 0.0)

        wb = {}
        x_sb = {}

        def load_w(c):
            n, g = loads[c]
            cols = GROUP_HEADS[n] * D
            c0 = first_head[n] * D
            wb[(n, g)] = wbytes.tile([P, PACK, cols], U8, name="wb", tag="wb")
            nc.sync.dma_start(out=wb[(n, g)][:], in_=w_view[g][:, :, c0:c0 + cols])

        def load_x(g):
            x_sb[g] = const.tile([P, BATCH, 512], BF16, name="x_sb_%d" % g)
            nc.sync.dma_start(out=x_sb[g][:], in_=x_view[g])

        for c in range(0, 4):
            load_w(c)
        nc.sync.dma_start(out=bias_raw[0:HEADS, :], in_=b_qk.rearrange("(c d) -> c d", d=D))
        load_x(0)
        load_x(1)
        for c in range(4, 8):
            load_w(c)
        load_x(2)
        load_x(3)
        for c in range(8, LOAD_LEAD):
            load_w(c)

        junk1 = const.tile([P, 1], F32, name="junk1")
        nc.scalar.activation(out=junk1[:], in_=zero1[:], func=ACT.Sin)

        ident2 = const.tile([P, D + D // 2], F32, name="ident2")
        make_identity(nc, ident2[:, 0:D])
        nc.gpsimd.tensor_copy(out=ident2[:, D:D + D // 2], in_=ident2[:, 0:D // 2])
        ident = ident2[:, 0:D]
        swap = ident2[:, D // 2:D + D // 2]

        sh_i = const.tile([P, 7], I32, name="sh_i")
        nc.vector.tensor_tensor(out=sh_i[:], in0=d_i[:], in1=m_i[:], op=ALU.logical_shift_right)
        bit_i = const.tile([P, 7], I32, name="bit_i")
        nc.vector.tensor_single_scalar(out=bit_i[:], in_=sh_i[:], scalar=1, op=ALU.bitwise_and)
        bit_f = const.tile([P, 7], F32, name="bit_f")
        nc.vector.tensor_copy(out=bit_f[:], in_=bit_i[:])
        nbit_f = const.tile([P, 7], F32, name="nbit_f")
        nc.vector.tensor_scalar(out=nbit_f[:], in0=bit_f[:], scalar1=-1.0, scalar2=1.0, op0=ALU.mult, op1=ALU.add)
        fac = const.tile([P, 6], F32, name="fac")
        for m in range(6):
            nc.vector.scalar_tensor_tensor(
                out=fac[:, m:m + 1], in0=bit_f[:, m:m + 1], scalar=10000.0 ** (-(2.0 ** m) / 64.0),
                in1=nbit_f[:, m:m + 1], op0=ALU.mult, op1=ALU.add)
        om1 = const.tile([P, 1], F32, name="om1")
        nc.vector.tensor_scalar(out=om1[:], in0=fac[:, 0:1], scalar1=fac[:, 1:2], scalar2=fac[:, 2:3],
                                op0=ALU.mult, op1=ALU.mult)
        om2 = const.tile([P, 1], F32, name="om2")
        nc.vector.tensor_scalar(out=om2[:], in0=om1[:], scalar1=fac[:, 3:4], scalar2=fac[:, 4:5],
                                op0=ALU.mult, op1=ALU.mult)
        omega = const.tile([P, 1], F32, name="omega")
        nc.vector.tensor_scalar(out=omega[:], in0=om2[:], scalar1=fac[:, 5:6], scalar2=None, op0=ALU.mult)
        sgn = const.tile([P, 1], F32, name="sgn")
        nc.vector.tensor_scalar(out=sgn[:], in0=bit_f[:, 6:7], scalar1=-2.0, scalar2=1.0, op0=ALU.mult, op1=ALU.add)
        theta = const.tile([P, T], F32, name="theta")
        nc.vector.tensor_scalar(out=theta[:], in0=t_i[:], scalar1=omega[:, 0:1], scalar2=None, op0=ALU.mult)
        k_i = const.tile([P, T], I32, name="k_i")
        nc.vector.tensor_scalar(out=k_i[:], in0=theta[:], scalar1=1.0 / TWO_PI, scalar2=None, op0=ALU.mult)
        k_f = const.tile([P, T], F32, name="k_f")
        nc.vector.tensor_copy(out=k_f[:], in_=k_i[:])
        ph = [const.tile([P, T], F32, name="ph_%d" % i) for i in range(3)]
        nc.vector.scalar_tensor_tensor(out=ph[0][:], in0=k_f[:], scalar=-C1, in1=theta[:], op0=ALU.mult, op1=ALU.add)
        nc.vector.scalar_tensor_tensor(out=ph[1][:], in0=k_f[:], scalar=-C2, in1=ph[0][:], op0=ALU.mult, op1=ALU.add)
        nc.vector.scalar_tensor_tensor(out=ph[2][:], in0=k_f[:], scalar=-C3, in1=ph[1][:], op0=ALU.mult, op1=ALU.add)
        phi = ph[2]
        aphi = const.tile([P, T], F32, name="aphi")
        nc.vector.scalar_tensor_tensor(out=aphi[:], in0=phi[:], scalar=-1.0, in1=phi[:], op0=ALU.mult, op1=ALU.max)
        bias_f = const.tile([P, D], F32, name="bias_f")

        trig = const.tile([P, 2, BATCH, T], F32, name="trig")
        bias_sb = const.tile([P, HEADS], F32, name="bias_sb")

        def trig_tables():
            nc.scalar.activation(out=trig[:, 0, :, :], in_=aphi[:].unsqueeze(1).to_broadcast([P, BATCH, T]), func=ACT.Sin,
                                 bias=math.pi / 2.0, scale=-1.0)
            nc.scalar.activation(out=trig[:, 1, :, :], in_=phi[:].unsqueeze(1).to_broadcast([P, BATCH, T]), func=ACT.Sin,
                                 scale=sgn[:, 0:1])

        x_codes = const.tile([P, PASSES, TOK], U32, name="x_codes", align_bytes=64)
        x_scl = const.tile([P, PASSES, TOK], U8, name="x_scl", align_bytes=64)

        xg = {}
        bias_t = {}

        def bias_turn():
            nc.vector.tensor_copy(out=bias_f[:], in_=bias_raw[:])
            bias_t[0] = psum_tr.tile([P, 512], F32, name="bt", tag="tr")
            nc.tensor.transpose(out=bias_t[0][:, 0:D], in_=bias_f[:], identity=ident)

        def bias_keep():
            nc.vector.tensor_copy(out=bias_sb[:], in_=bias_t[0][:, 0:HEADS])

        def x_turn(g):
            xg[g] = const.tile([P, TOK, PACK], BF16, name="xg_%d" % g, align_bytes=64)
            xg_w = xg[g][:].rearrange("p r j -> p (r j)").bitcast(F32).rearrange(
                "p (h b r u) -> p h b r u", h=2, b=2, u=2)
            for half in range(2):
                xt = psum_tr.tile([P, 2, 2, T], F32, name="xt", tag="tr")
                for bb in range(2):
                    words = x_sb[g][:, 2 * half + bb, :].bitcast(F32)
                    for u in range(2):
                        nc.tensor.transpose(out=xt[:, bb, u, :], in_=words[:, u:256:2], identity=ident)
                nc.scalar.copy(out=xg_w[:, half], in_=xt[:].rearrange("p b u r -> p b r u"))

        def x_quant(g):
            nc.vector.quantize_mx(out=x_codes[:, g, :].bitcast(FP8X4), scales=x_scl[:, g, :],
                                  in_=xg[g][:].rearrange("p r j -> p (r j)"))

        planes = {}
        inter = {}
        w_codes = {}
        w_scl = {}

        def widen(c, spare):
            n, passes = chunks[c]
            cols = GROUP_HEADS[n] * D
            planes[c] = work.tile([P, PACK, len(passes) * cols], BF16, name="planes", tag="planes", bufs=8)
            for i in range(len(passes)):
                g = passes[i]
                load = PASSES * n + g
                v_planes = 1 if (load < 8 or (load % 4 == 0 and load < 32)) else 0
                if load < 8 and load % 2 == 0:
                    v_planes = 2
                if len(passes) == 2:
                    v_planes += (spare + 1 - i) // 2
                for t in range(PACK - v_planes):
                    nc.scalar.activation(out=planes[c][:, t, i * cols:(i + 1) * cols],
                                         in_=wb[(n, g)][:, t, :].bitcast(FP8), func=ACT.Copy,
                                         scale=wsc[:, g, t:t + 1])
                for t in range(PACK - v_planes, PACK):
                    nc.vector.tensor_scalar(out=planes[c][:, t, i * cols:(i + 1) * cols],
                                            in0=wb[(n, g)][:, t, :].bitcast(FP8),
                                            scalar1=wsc[:, g, t:t + 1], scalar2=None, op0=ALU.mult)

        g_cols = {}
        s_cols = {}

        def interleave_g(c, ropes):
            n, passes = chunks[c]
            cols = len(passes) * GROUP_HEADS[n] * D
            inter[c] = work.tile([P, cols, PACK], BF16, name="inter", tag="inter", bufs=2, align_bytes=64)
            g_cols[c] = min(G_COLS[min(ropes, 2)], cols)
            s_cols[c] = 0
            lo = g_cols[c]
            if lo > 0:
                nc.gpsimd.tensor_scalar(out=inter[c][:, 0:lo, :],
                                        in0=planes[c][:, :, 0:lo].rearrange("p t n -> p n t"),
                                        scalar1=1.0, scalar2=0.0, op0=ALU.mult, op1=ALU.add)
            if s_cols[c] > 0:
                nc.scalar.copy(out=inter[c][:, lo:lo + s_cols[c], :],
                               in_=planes[c][:, :, lo:lo + s_cols[c]].rearrange("p t n -> p n t"))

        def interleave_v(c):
            lo = g_cols[c] + s_cols[c]
            if lo < inter[c].shape[1]:
                nc.vector.tensor_copy(out=inter[c][:, lo:, :].rearrange("p (c i) t -> p c t i", i=8),
                                      in_=planes[c][:, :, lo:].rearrange("p t (c i) -> p c t i", i=8))

        def quantize(c):
            n, passes = chunks[c]
            cols = GROUP_HEADS[n] * D
            g0, g1 = passes[0], passes[-1] + 1
            if g0 == 0:
                w_codes[n] = work.tile([P, PASSES, cols], U32, name="w_codes", tag="w_codes", bufs=4, align_bytes=64)
                w_scl[n] = work.tile([P, PASSES, cols], U8, name="w_scl", tag="w_scl", bufs=4, align_bytes=64)
            nc.vector.quantize_mx(out=w_codes[n][:, g0:g1, :].rearrange("p g c -> p (g c)").bitcast(FP8X4),
                                  scales=w_scl[n][:, g0:g1, :].rearrange("p g c -> p (g c)"),
                                  in_=inter[c][:].rearrange("p n t -> p (n t)"))

        acc = {}
        rot = {}
        turned = {}

        def project(k, passes):
            n = head_group[k]
            c0 = (k - first_head[n]) * D
            if passes[0] == 0:
                acc[k] = psum_acc.tile([P, TOK], F32, name="acc", tag="acc")
            for g in passes:
                nc.tensor.matmul_mx(
                    out=acc[k][:],
                    lhsT=w_codes[n][:, g, c0:c0 + D].bitcast(FP8X4), lhsT_scale=w_scl[n][:, g, c0:c0 + D],
                    rhs=x_codes[:, g, :].bitcast(FP8X4), rhs_scale=x_scl[:, g, :],
                    start=(g == 0), stop=(g == PASSES - 1))

        def rope(k, b0, b1):
            if b0 == 0:
                rot[k] = work.tile([P, 2, TOK], F32, name="rot", tag="rot", bufs=4)
            lo, hi = b0 * T, b1 * T
            nc.vector.scalar_tensor_tensor(out=rot[k][:, :, lo:hi],
                                           in0=acc[k][:, lo:hi].unsqueeze(1).to_broadcast([P, 2, hi - lo]),
                                           scalar=bias_sb[:, k:k + 1],
                                           in1=trig[:].rearrange("p c b t -> p c (b t)")[:, :, lo:hi],
                                           op0=ALU.add, op1=ALU.mult)

        def turn(k, b0, b1, own_bank):
            if b0 == 0 or own_bank:
                turned[(k, b0)] = psum_tr.tile([P, BATCH, D], F32, name="turned", tag="tr")
            bank = turned[(k, b0)] if own_bank else turned[(k, 0)]
            for b in range(b0, b1):
                nc.tensor.matmul(out=bank[:, b, :], lhsT=rot[k][:, 0, b * T:(b + 1) * T], rhs=ident,
                                 is_transpose=True, start=True, stop=False)
                nc.tensor.matmul(out=bank[:, b, :], lhsT=rot[k][:, 1, b * T:(b + 1) * T], rhs=swap,
                                 is_transpose=True, start=False, stop=True)

        def leave(k, b0, b1):
            o_sb = work.tile([P, BATCH, D], F32, name="o_sb", tag="o_sb", bufs=6)
            nc.scalar.copy(out=o_sb[:, b0:b1, :], in_=turned[(k, b0)][:, b0:b1, :])
            dst = out_0 if k < HEADS // 2 else out_1
            nc.sync.dma_start(out=dst[b0:b1, k % (HEADS // 2), :, :].rearrange("b t d -> t b d"), in_=o_sb[:, b0:b1, :])

        state = {"ready": 0, "projected": 0, "slots": 0}
        held = []

        def slot(hold):
            k = state["slots"]
            ahead = []
            while state["projected"] < min(state["ready"], k + MM_AHEAD + 1):
                h = state["projected"]
                project(h, (0, 1, 2, 3))
                state["projected"] += 1
            if k < HEADS - 1:
                rope(k, 0, BATCH)
                held.append(k)
                if not hold:
                    for h in held:
                        turn(h, 0, BATCH, False)
                    for h in held:
                        if h >= EVAC_LAG:
                            leave(h - EVAC_LAG, 0, BATCH)
                    held.clear()
            else:
                rope(k, 0, 2)
                turn(k, 0, 2, True)
                leave(k - 2, 0, BATCH)
                rope(k, 2, BATCH)
                turn(k, 2, BATCH, True)
                leave(k - 1, 0, BATCH)
                leave(k, 0, 2)
                leave(k, 2, BATCH)
            state["slots"] += 1

        def ropes_due(s):
            due = 0
            for n in range(len(GROUP_HEADS)):
                spread = group_chunks[min(n + 1, len(GROUP_HEADS) - 1)]
                due += (GROUP_HEADS[n] * min(max(s - (last_chunk[n] + 2), 0), spread)) // spread
            return due

        state["loaded"] = LOAD_LEAD
        for s in range(n_chunks + 2):
            while state["loaded"] < min(len(loads), loads_through[min(s, n_chunks - 1)] + LOAD_LEAD):
                load_w(state["loaded"])
                state["loaded"] += 1
            due = ropes_due(s)
            if s == 0:
                widen(0, 0)
            if s + 1 < n_chunks:
                widen(s + 1, (2 - min(due - state["slots"], 2)) if len(chunks[s][1]) == 2 else 0)
            if s == 1:
                trig_tables()
            if s == 6:
                bias_turn()
            if 2 <= s < 2 + PASSES:
                x_turn(s - 2)
            if 1 <= s <= n_chunks:
                interleave_v(s - 1)
            if s >= 2:
                quantize(s - 2)
                n, passes = chunks[s - 2]
                if passes[-1] == PASSES - 1:
                    state["ready"] += GROUP_HEADS[n]
            if s == 7:
                bias_keep()
            if 3 <= s < 3 + PASSES:
                x_quant(s - 3)
            if s < n_chunks:
                interleave_g(s, due - state["slots"])
            while state["slots"] < due:
                slot(state["slots"] + 1 < due)
        while state["slots"] < HEADS:
            slot(False)
